import numpy as np
import ml_dtypes


def mxq(x, axis, fmt="e4m3"):
    dtype, down = {"e4m3": (ml_dtypes.float8_e4m3fn, 7), "e5m2": (ml_dtypes.float8_e5m2, 14)}[fmt]
    v = np.moveaxis(np.asarray(x, np.float32).astype(ml_dtypes.bfloat16).astype(np.float64), axis, -1)
    blocks = v.reshape(v.shape[:-1] + (-1, 32))
    amax = np.abs(blocks).max(-1, keepdims=True)
    byte = np.maximum(np.where(amax > 0, np.frexp(amax)[1] - 1 + 127, 0) - down, 1)
    scale = np.exp2(byte - 127.0)
    codes = (blocks / scale).astype(np.float32).astype(dtype).astype(np.float64)
    return np.moveaxis((codes * scale).reshape(v.shape), -1, axis)


WIDE = False


def mx_kscale(k):
    if not WIDE:
        return np.ones(k)
    levels = np.array([10, -10, 5, -5, 0])
    a = np.random.permutation(np.resize(levels, k // 512 * 4)).reshape(k // 512, 4)
    idx = np.arange(k)
    return np.exp2(a[idx // 512, idx % 128 // 32])


BF16 = ml_dtypes.bfloat16


def bf(x):
    return np.asarray(x, np.float32).astype(BF16)


def f64(x):
    return np.asarray(x).astype(np.float64)


E2M1 = np.array([0.0, 0.5, 1.0, 1.5, 2.0, 3.0, 4.0, 6.0, -0.0, -0.5, -1.0, -1.5, -2.0, -3.0, -4.0, -6.0])


def pack_weight(w, fmt):
    k, n = w.shape
    w = f64(bf(w)).reshape(k // 32, 32, n)
    amax = np.abs(w).max(1)
    if fmt == "e4m3":
        byte = np.frexp(amax)[1] - 1 + 127 - 7
    else:
        mant, ex = np.frexp(amax / 6.0)
        byte = np.where(mant > 0.5, ex, ex - 1) + 127
    byte = np.clip(np.where(amax > 0, byte, 1), 1, 254)
    scaled = (w * np.exp2(127.0 - byte)[:, None, :]).reshape(k, n).astype(np.float32)
    by_word = np.ascontiguousarray(scaled.reshape(k // 512, 128, 4, n).transpose(0, 1, 3, 2))
    if fmt == "e4m3":
        words = by_word.astype(ml_dtypes.float8_e4m3fn).view(np.uint8)
    else:
        c = by_word.astype(ml_dtypes.float4_e2m1fn).view(np.uint8) & 0xF
        words = c[..., 0::2] | (c[..., 1::2] << 4)
    return np.ascontiguousarray(words), np.ascontiguousarray(byte.astype(np.uint8).reshape(k // 512, 16, n))


def unpack_weight(words, scales, fmt):
    g, p, n, _ = words.shape
    if fmt == "e4m3":
        vals = np.ascontiguousarray(words).view(ml_dtypes.float8_e4m3fn).astype(np.float64)
    else:
        nib = np.empty((g, p, n, 4), np.uint8)
        nib[..., 0::2] = words & 0xF
        nib[..., 1::2] = words >> 4
        vals = E2M1[nib]
    vals = vals * np.repeat(np.exp2(scales.astype(np.float64) - 127.0), 8, axis=1)[..., None]
    return vals.transpose(0, 1, 3, 2).reshape(g * 512, n)

def pack4(w):
    words, scales = pack_weight(w, "e2m1")
    return words.reshape(words.shape[0], 128, -1), scales


def unpack4(words, scales):
    return unpack_weight(words.reshape(words.shape[0], 128, -1, 2), scales, "e2m1")


B, Nb1, Nw1, Nb2x, Nb2y, Nw2x, Nw2y, R, C = 128, 4, 16, 4, 2, 16, 16, 128, 2
J1 = Nb1 * Nb1
K1 = C * Nw1 * Nw1
J3 = Nb2x * Nb2y
L1 = J3 * R
J2 = J3 * J1


def setup_inputs():
    s = mx_kscale(K1)
    sx = s.reshape(Nw1, Nw1, C)[:, None, :, :]
    x = np.random.standard_normal((B, Nb1, Nw1, Nb1, Nw1, C)) * sx
    k1 = np.random.standard_normal((J1, K1, L1)) / np.sqrt(K1) / s[None, :, None]
    k1_words, k1_scales = pack4(k1.reshape(-1, L1))
    return {"x": bf(x.reshape(B, Nb1 * Nw1 * Nb1 * Nw1, C)),
            "k1_words": k1_words,
            "k1_scales": k1_scales,
            "b1": bf(np.random.standard_normal((1, J1, L1)) * 0.3)}


def reference(x, k1_words, k1_scales, b1):
    h = f64(x).reshape(B, Nb1, Nw1, Nb1, Nw1, C).transpose(0, 1, 3, 2, 4, 5).reshape(B, J1, K1)
    hq = mxq(h, 2, "e4m3").transpose(1, 0, 2)
    k1 = unpack4(k1_words, k1_scales).reshape(J1, K1, L1)
    y = (hq @ k1).transpose(1, 0, 2) + f64(b1)
    y = y.reshape(B, J1, J3, R).transpose(0, 3, 1, 2)
    return y.reshape(B, J2, R)

@@ -1,0 +1,137 @@
+import concourse.mybir as mybir
+from concourse.masks import make_identity
+
+F32 = mybir.dt.float32
+BF16 = mybir.dt.bfloat16
+I32 = mybir.dt.int32
+U32 = mybir.dt.uint32
+U8 = mybir.dt.uint8
+FP8X4 = mybir.dt.float8_e4m3fn_x4
+FP4X4 = mybir.dt.float4_e2m1fn_x4
+
+P = 128
+GRID = 4
+SIDE = 16
+ROW = 32
+BLOCKS = GRID * GRID
+K = SIDE * ROW
+L = 1024
+R = 128
+M_OUT = L // R
+BANK = 512
+M_BANK = BANK // R
+HALVES = L // BANK
+R_CHUNK = 8
+
+FLOPS = 2 * P * K * L * BLOCKS
+
+
+def tile_switchnet_fstar_pa_e_kernel(tc, x, k1_words, k1_scales, b1, out):
+    nc = tc.nc
+    with tc.tile_pool(name="keep", bufs=1) as keep, tc.tile_pool(name="stage", bufs=2) as stage, tc.psum_pool(
+        name="psum_x", bufs=2
+    ) as psum_x, tc.psum_pool(name="psum_y", bufs=4) as psum_y, tc.psum_pool(name="psum_b", bufs=2) as psum_b:
+        ident_f32 = keep.tile([P, P], F32)
+        make_identity(nc, ident_f32[:])
+        ident_bf16 = keep.tile([P, P], BF16)
+        make_identity(nc, ident_bf16[:])
+
+        w_words = keep.tile([P, BLOCKS, 2 * L], U8, align_bytes=64)
+        w_scales = keep.tile([P, BLOCKS, L], U8, align_bytes=64)
+        h_words = keep.tile([P, BLOCKS, P], U32, align_bytes=64)
+        h_scales = keep.tile([P, BLOCKS, P], U8, align_bytes=64)
+        b1_rows = keep.tile([P, R], BF16)
+        out_sb = keep.tile([P, R, BLOCKS * M_OUT], F32)
+
+        nc.vector.memset(w_scales[:].rearrange("p g n -> p (g n)").bitcast(I32), 0)
+
+        x_flat = x.rearrange("b g c -> b (g c)")
+        x_rows = []
+        for br in range(GRID):
+            x_raw = keep.tile([P, SIDE, GRID, ROW], BF16, name="x_raw%d" % br)
+            nc.sync.dma_start(
+                out=x_raw[:].rearrange("p r c k -> p (r c k)"),
+                in_=x_flat[:, br * GRID * K : (br + 1) * GRID * K],
+            )
+            x_rows.append(x_raw)
+
+        scales_i32 = k1_scales.bitcast(I32)
+        for g0 in range(0, BLOCKS, BLOCKS // 2):
+            g1 = g0 + BLOCKS // 2
+            for q in range(8):
+                first = 32 * (q // 4) + q % 4
+                nc.sync.dma_start(
+                    out=w_scales[first:P:64, g0:g1, :].bitcast(I32),
+                    in_=scales_i32[g0:g1, q:16:8, :].rearrange("g h n -> h g n"),
+                )
+
+        words_i32 = k1_words.bitcast(I32)
+        for j in range(0, BLOCKS, 2):
+            nc.sync.dma_start(
+                out=w_words[:, j : j + 2, :].bitcast(I32),
+                in_=words_i32[j : j + 2].rearrange("g p n -> p g n"),
+            )
+
+        nc.scalar.dma_start(out=b1_rows[:], in_=b1.rearrange("o j (m r) -> (o j m) r", r=R))
+
+        for br in range(GRID):
+            windows = stage.tile([P, GRID, SIDE, ROW], BF16)
+            nc.vector.tensor_copy(out=windows[:], in_=x_rows[br][:].rearrange("p r c k -> p c r k"))
+            pairs = windows[:].rearrange("p c r k -> p (c r k)").bitcast(F32)
+
+            grouped = stage.tile([P, GRID, P, 4], BF16, align_bytes=64)
+            for c0 in range(0, GRID, 2):
+                xt = psum_x.tile([P, 2, 2, P], F32)
+                for c in range(2):
+                    for u in range(2):
+                        first = (c0 + c) * (K // 2) + u
+                        nc.tensor.transpose(
+                            out=xt[:, c, u, :],
+                            in_=pairs[:, first : (c0 + c + 1) * (K // 2) : 2],
+                            identity=ident_f32[:],
+                        )
+                nc.scalar.copy(
+                    out=grouped[:, c0 : c0 + 2, :, :]
+                    .rearrange("p c b t -> p (c b t)")
+                    .bitcast(F32)
+                    .rearrange("p (c b u) -> p c b u", c=2, u=2),
+                    in_=xt[:].rearrange("p c u b -> p c b u"),
+                )
+            blocks = slice(br * GRID, (br + 1) * GRID)
+            nc.vector.quantize_mx(
+                out=h_words[:, blocks, :].rearrange("p j b -> p (j b)").bitcast(FP8X4),
+                scales=h_scales[:, blocks, :].rearrange("p j b -> p (j b)"),
+                in_=grouped[:].rearrange("p c b t -> p (c b t)"),
+            )
+
+        for j in range(BLOCKS):
+            for half in range(HALVES):
+                y = psum_y.tile([P, BANK], F32)
+                nc.tensor.matmul_mx(
+                    out=y[:],
+                    lhsT=h_words[:, j, :].bitcast(FP8X4),
+                    lhsT_scale=h_scales[:, j, :],
+                    rhs=w_words[:, j, 2 * BANK * half : 2 * BANK * (half + 1)].bitcast(FP4X4),
+                    rhs_scale=w_scales[:, j, BANK * half : BANK * (half + 1)],
+                    start=True,
+                    stop=True,
+                )
+                first = M_OUT * j + M_BANK * half
+                switched = out_sb[:, :, first : first + M_BANK]
+                by_r = y[:].rearrange("p (m r) -> p r m", m=M_BANK)
+                if j % 2 == 0:
+                    nc.vector.tensor_copy(out=switched, in_=by_r)
+                else:
+                    nc.scalar.copy(out=switched, in_=by_r)
+
+        for r0 in range(0, R, R_CHUNK):
+            bias = psum_b.tile([P, R_CHUNK, P], BF16)
+            for i in range(R_CHUNK):
+                nc.tensor.transpose(
+                    out=bias[:, i, :],
+                    in_=b1_rows[:, r0 + i : r0 + i + 1].to_broadcast([P, P]),
+                    identity=ident_bf16[:],
+                )
+            rows = out_sb[:, r0 : r0 + R_CHUNK, :]
+            nc.vector.tensor_tensor(out=rows, in0=bias[:], in1=rows, op=mybir.AluOpType.add)
+            nc.sync.dma_start(out=out[:, r0 : r0 + R_CHUNK, :], in_=rows)

@@ -8,6 +8,7 @@ U32 = mybir.dt.uint32
 U8 = mybir.dt.uint8
 FP8X4 = mybir.dt.float8_e4m3fn_x4
 FP4X4 = mybir.dt.float4_e2m1fn_x4
+ADD = mybir.AluOpType.add
 
 P = 128
 GRID = 4
@@ -15,12 +16,14 @@ SIDE = 16
 ROW = 32
 BLOCKS = GRID * GRID
 K = SIDE * ROW
-L = 1024
 R = 128
-M_OUT = L // R
+M_OUT = 8
+L = M_OUT * R
 BANK = 512
 M_BANK = BANK // R
 HALVES = L // BANK
+ODD = BLOCKS // 2
+R_HALF = R // 2
 R_CHUNK = 8
 
 FLOPS = 2 * P * K * L * BLOCKS
@@ -29,8 +32,8 @@ FLOPS = 2 * P * K * L * BLOCKS
 def tile_switchnet_fstar_pa_e_kernel(tc, x, k1_words, k1_scales, b1, out):
     nc = tc.nc
     with tc.tile_pool(name="keep", bufs=1) as keep, tc.tile_pool(name="stage", bufs=2) as stage, tc.psum_pool(
-        name="psum_x", bufs=2
-    ) as psum_x, tc.psum_pool(name="psum_y", bufs=4) as psum_y, tc.psum_pool(name="psum_b", bufs=2) as psum_b:
+        name="psum", bufs=8
+    ) as psum, tc.manual_schedule():
         ident_f32 = keep.tile([P, P], F32)
         make_identity(nc, ident_f32[:])
         ident_bf16 = keep.tile([P, P], BF16)
@@ -40,10 +43,21 @@ def tile_switchnet_fstar_pa_e_kernel(tc, x, k1_words, k1_scales, b1, out):
         w_scales = keep.tile([P, BLOCKS, L], U8, align_bytes=64)
         h_words = keep.tile([P, BLOCKS, P], U32, align_bytes=64)
         h_scales = keep.tile([P, BLOCKS, P], U8, align_bytes=64)
-        b1_rows = keep.tile([P, R], BF16)
         out_sb = keep.tile([P, R, BLOCKS * M_OUT], F32)
+        bias_even = keep.tile([P, ODD, L], BF16)
+        b1_two_rows = keep.tile([P, 2 * R], BF16)
+        b1_words = keep.tile([P, P // 2], F32)
+        b1_odd = keep.tile([P, R_HALF], BF16)
 
         nc.vector.memset(w_scales[:].rearrange("p g n -> p (g n)").bitcast(I32), 0)
+        nc.gpsimd.memset(b1_two_rows[P // 2 : P, :], 0.0)
+
+        nc.scalar.dma_start(
+            out=b1_two_rows[0 : P // 2, :], in_=b1.rearrange("o j (i w) -> (o j i) w", w=2 * R)
+        )
+        b1_by_parity = b1.rearrange("o (j2 par) (m rh c) -> o par rh j2 m c", par=2, m=M_OUT, rh=2)
+        for rh in range(2):
+            nc.scalar.dma_start(out=b1_odd[R_HALF * rh : R_HALF * (rh + 1), :], in_=b1_by_parity[0, 1, rh])
 
         x_flat = x.rearrange("b g c -> b (g c)")
         x_rows = []
@@ -72,22 +86,21 @@ def tile_switchnet_fstar_pa_e_kernel(tc, x, k1_words, k1_scales, b1, out):
                 in_=words_i32[j : j + 2].rearrange("g p n -> p g n"),
             )
 
-        nc.scalar.dma_start(out=b1_rows[:], in_=b1.rearrange("o j (m r) -> (o j m) r", r=R))
-
-        for br in range(GRID):
-            windows = stage.tile([P, GRID, SIDE, ROW], BF16)
+        def gather_windows(br):
+            windows = stage.tile([P, GRID, SIDE, ROW], BF16, name="windows")
             nc.vector.tensor_copy(out=windows[:], in_=x_rows[br][:].rearrange("p r c k -> p c r k"))
-            pairs = windows[:].rearrange("p c r k -> p (c r k)").bitcast(F32)
+            return windows
 
-            grouped = stage.tile([P, GRID, P, 4], BF16, align_bytes=64)
+        def transpose_windows(windows):
+            pairs = windows[:].rearrange("p c r k -> p (c r k)").bitcast(F32)
+            grouped = stage.tile([P, GRID, P, 4], BF16, align_bytes=64, name="grouped")
             for c0 in range(0, GRID, 2):
-                xt = psum_x.tile([P, 2, 2, P], F32)
+                xt = psum.tile([P, 2, 2, P], F32, name="xt", tag="bank")
                 for c in range(2):
                     for u in range(2):
-                        first = (c0 + c) * (K // 2) + u
                         nc.tensor.transpose(
                             out=xt[:, c, u, :],
-                            in_=pairs[:, first : (c0 + c + 1) * (K // 2) : 2],
+                            in_=pairs[:, (c0 + c) * (K // 2) + u : (c0 + c + 1) * (K // 2) : 2],
                             identity=ident_f32[:],
                         )
                 nc.scalar.copy(
@@ -97,6 +110,29 @@ def tile_switchnet_fstar_pa_e_kernel(tc, x, k1_words, k1_scales, b1, out):
                     .rearrange("p (c b u) -> p c b u", c=2, u=2),
                     in_=xt[:].rearrange("p c u b -> p c b u"),
                 )
+            return grouped
+
+        def spread_even_bias(j):
+            spread = psum.tile([P, M_BANK, P], F32, name="spread", tag="bank")
+            for i in range(M_BANK):
+                col = M_BANK * j + i
+                nc.tensor.transpose(
+                    out=spread[:, i, :], in_=b1_words[:, col : col + 1].to_broadcast([P, P]), identity=ident_f32[:]
+                )
+            nc.scalar.copy(out=bias_even[:, j // 2, :].bitcast(F32), in_=spread[:].rearrange("p i w -> p (i w)"))
+
+        b1_t = psum.tile([P, P], F32, name="b1_t", tag="bank")
+        nc.tensor.transpose(out=b1_t[:], in_=b1_two_rows[:].bitcast(F32), identity=ident_f32[:])
+        nc.scalar.copy(out=b1_words[:], in_=b1_t[:, 0 : P // 2])
+
+        windows_next = gather_windows(0)
+        for br in range(GRID):
+            windows = windows_next
+            if br + 1 < GRID:
+                windows_next = gather_windows(br + 1)
+            grouped = transpose_windows(windows)
+            spread_even_bias(GRID * br)
+            spread_even_bias(GRID * br + 2)
             blocks = slice(br * GRID, (br + 1) * GRID)
             nc.vector.quantize_mx(
                 out=h_words[:, blocks, :].rearrange("p j b -> p (j b)").bitcast(FP8X4),
@@ -106,7 +142,7 @@ def tile_switchnet_fstar_pa_e_kernel(tc, x, k1_words, k1_scales, b1, out):
 
         for j in range(BLOCKS):
             for half in range(HALVES):
-                y = psum_y.tile([P, BANK], F32)
+                y = psum.tile([P, BANK], F32, name="y", tag="bank")
                 nc.tensor.matmul_mx(
                     out=y[:],
                     lhsT=h_words[:, j, :].bitcast(FP8X4),
@@ -120,18 +156,29 @@ def tile_switchnet_fstar_pa_e_kernel(tc, x, k1_words, k1_scales, b1, out):
                 switched = out_sb[:, :, first : first + M_BANK]
                 by_r = y[:].rearrange("p (m r) -> p r m", m=M_BANK)
                 if j % 2 == 0:
-                    nc.vector.tensor_copy(out=switched, in_=by_r)
+                    bias_by_r = bias_even[:, j // 2, BANK * half : BANK * (half + 1)].rearrange(
+                        "p (m r) -> p r m", m=M_BANK
+                    )
+                    nc.vector.tensor_tensor(out=switched, in0=by_r, in1=bias_by_r, op=ADD)
                 else:
                     nc.scalar.copy(out=switched, in_=by_r)
 
-        for r0 in range(0, R, R_CHUNK):
-            bias = psum_b.tile([P, R_CHUNK, P], BF16)
+        for c0 in range(0, R_HALF, R_CHUNK):
+            spread_odd = psum.tile([P, R_CHUNK, 2, R_HALF], BF16, name="spread_odd", tag="bank")
             for i in range(R_CHUNK):
                 nc.tensor.transpose(
-                    out=bias[:, i, :],
-                    in_=b1_rows[:, r0 + i : r0 + i + 1].to_broadcast([P, P]),
+                    out=spread_odd[:, i, :, :].rearrange("p rh w -> p (rh w)"),
+                    in_=b1_odd[:, c0 + i : c0 + i + 1].to_broadcast([P, P]),
                     identity=ident_bf16[:],
                 )
-            rows = out_sb[:, r0 : r0 + R_CHUNK, :]
-            nc.vector.tensor_tensor(out=rows, in0=bias[:], in1=rows, op=mybir.AluOpType.add)
-            nc.sync.dma_start(out=out[:, r0 : r0 + R_CHUNK, :], in_=rows)
+            for rh in range(2):
+                r0 = R_HALF * rh + c0
+                rows = out_sb[:, r0 : r0 + R_CHUNK, :]
+                odd_columns = rows.rearrange("p r (j2 par m) -> p r j2 par m", par=2, m=M_OUT)[:, :, :, 1, :]
+                nc.vector.tensor_tensor(
+                    out=odd_columns,
+                    in0=spread_odd[:, :, rh, :].rearrange("p c (j2 m) -> p c j2 m", m=M_OUT),
+                    in1=odd_columns,
+                    op=ADD,
+                )
+                nc.sync.dma_start(out=out[:, r0 : r0 + R_CHUNK, :], in_=rows)

@@ -80,11 +80,8 @@ def tile_switchnet_fstar_pa_e_kernel(tc, x, k1_words, k1_scales, b1, out):
                 )
 
         words_i32 = k1_words.bitcast(I32)
-        for j in range(0, BLOCKS, 2):
-            nc.sync.dma_start(
-                out=w_words[:, j : j + 2, :].bitcast(I32),
-                in_=words_i32[j : j + 2].rearrange("g p n -> p g n"),
-            )
+        for j in range(BLOCKS):
+            nc.sync.dma_start(out=w_words[:, j, :].bitcast(I32), in_=words_i32[j])
 
         def gather_windows(br):
             windows = stage.tile([P, GRID, SIDE, ROW], BF16, name="windows")
@@ -130,9 +127,9 @@ def tile_switchnet_fstar_pa_e_kernel(tc, x, k1_words, k1_scales, b1, out):
             windows = windows_next
             if br + 1 < GRID:
                 windows_next = gather_windows(br + 1)
-            grouped = transpose_windows(windows)
             spread_even_bias(GRID * br)
             spread_even_bias(GRID * br + 2)
+            grouped = transpose_windows(windows)
             blocks = slice(br * GRID, (br + 1) * GRID)
             nc.vector.quantize_mx(
                 out=h_words[:, blocks, :].rearrange("p j b -> p (j b)").bitcast(FP8X4),

@@ -22,9 +22,10 @@ L = M_OUT * R
 BANK = 512
 M_BANK = BANK // R
 HALVES = L // BANK
-ODD = BLOCKS // 2
-R_HALF = R // 2
+R_LOW = R // 2
+R_FIRST = 16
 R_CHUNK = 8
+R_STORE = 32
 
 FLOPS = 2 * P * K * L * BLOCKS
 
@@ -44,20 +45,20 @@ def tile_switchnet_fstar_pa_e_kernel(tc, x, k1_words, k1_scales, b1, out):
         h_words = keep.tile([P, BLOCKS, P], U32, align_bytes=64)
         h_scales = keep.tile([P, BLOCKS, P], U8, align_bytes=64)
         out_sb = keep.tile([P, R, BLOCKS * M_OUT], F32)
-        bias_even = keep.tile([P, ODD, L], BF16)
-        b1_two_rows = keep.tile([P, 2 * R], BF16)
-        b1_words = keep.tile([P, P // 2], F32)
-        b1_odd = keep.tile([P, R_HALF], BF16)
+        bias_low = keep.tile([P, BLOCKS, M_OUT * R_LOW], BF16)
+        b1_four_rows = keep.tile([P, M_BANK * R_LOW], BF16)
+        b1_words = keep.tile([P, P // M_BANK], F32)
+        b1_high = keep.tile([P, R - R_LOW], BF16)
 
         nc.vector.memset(w_scales[:].rearrange("p g n -> p (g n)").bitcast(I32), 0)
-        nc.gpsimd.memset(b1_two_rows[P // 2 : P, :], 0.0)
+        nc.gpsimd.memset(b1_four_rows[P // 4 : P // 2, :], 0.0)
+        nc.gpsimd.memset(b1_four_rows[P // 2 : P, :], 0.0)
 
         nc.scalar.dma_start(
-            out=b1_two_rows[0 : P // 2, :], in_=b1.rearrange("o j (i w) -> (o j i) w", w=2 * R)
+            out=b1_four_rows[0 : P // M_BANK, :].rearrange("p (q c) -> p q c", q=M_BANK),
+            in_=b1.rearrange("o j (mh q rh c) -> o rh (j mh) q c", mh=HALVES, q=M_BANK, rh=2)[0, 0],
         )
-        b1_by_parity = b1.rearrange("o (j2 par) (m rh c) -> o par rh j2 m c", par=2, m=M_OUT, rh=2)
-        for rh in range(2):
-            nc.scalar.dma_start(out=b1_odd[R_HALF * rh : R_HALF * (rh + 1), :], in_=b1_by_parity[0, 1, rh])
+        nc.scalar.dma_start(out=b1_high[:], in_=b1.rearrange("o j (m rh c) -> o rh (j m) c", m=M_OUT, rh=2)[0, 1])
 
         x_flat = x.rearrange("b g c -> b (g c)")
         x_rows = []
@@ -109,26 +110,29 @@ def tile_switchnet_fstar_pa_e_kernel(tc, x, k1_words, k1_scales, b1, out):
                 )
             return grouped
 
-        def spread_even_bias(j):
+        def spread_low_bias(j):
             spread = psum.tile([P, M_BANK, P], F32, name="spread", tag="bank")
             for i in range(M_BANK):
-                col = M_BANK * j + i
+                col = HALVES * j + i
                 nc.tensor.transpose(
                     out=spread[:, i, :], in_=b1_words[:, col : col + 1].to_broadcast([P, P]), identity=ident_f32[:]
                 )
-            nc.scalar.copy(out=bias_even[:, j // 2, :].bitcast(F32), in_=spread[:].rearrange("p i w -> p (i w)"))
+            nc.scalar.copy(
+                out=bias_low[:, j : j + 2, :].rearrange("p j w -> p (j w)").bitcast(F32),
+                in_=spread[:].rearrange("p i w -> p (i w)"),
+            )
 
         b1_t = psum.tile([P, P], F32, name="b1_t", tag="bank")
-        nc.tensor.transpose(out=b1_t[:], in_=b1_two_rows[:].bitcast(F32), identity=ident_f32[:])
-        nc.scalar.copy(out=b1_words[:], in_=b1_t[:, 0 : P // 2])
+        nc.tensor.transpose(out=b1_t[:], in_=b1_four_rows[:].bitcast(F32), identity=ident_f32[:])
+        nc.scalar.copy(out=b1_words[:], in_=b1_t[:, 0 : P // M_BANK])
 
         windows_next = gather_windows(0)
         for br in range(GRID):
             windows = windows_next
             if br + 1 < GRID:
                 windows_next = gather_windows(br + 1)
-            spread_even_bias(GRID * br)
-            spread_even_bias(GRID * br + 2)
+            spread_low_bias(GRID * br)
+            spread_low_bias(GRID * br + 2)
             grouped = transpose_windows(windows)
             blocks = slice(br * GRID, (br + 1) * GRID)
             nc.vector.quantize_mx(
@@ -137,45 +141,60 @@ def tile_switchnet_fstar_pa_e_kernel(tc, x, k1_words, k1_scales, b1, out):
                 in_=grouped[:].rearrange("p c b t -> p (c b t)"),
             )
 
-        for j in range(BLOCKS):
-            for half in range(HALVES):
-                y = psum.tile([P, BANK], F32, name="y", tag="bank")
-                nc.tensor.matmul_mx(
-                    out=y[:],
-                    lhsT=h_words[:, j, :].bitcast(FP8X4),
-                    lhsT_scale=h_scales[:, j, :],
-                    rhs=w_words[:, j, 2 * BANK * half : 2 * BANK * (half + 1)].bitcast(FP4X4),
-                    rhs_scale=w_scales[:, j, BANK * half : BANK * (half + 1)],
-                    start=True,
-                    stop=True,
-                )
-                first = M_OUT * j + M_BANK * half
-                switched = out_sb[:, :, first : first + M_BANK]
-                by_r = y[:].rearrange("p (m r) -> p r m", m=M_BANK)
-                if j % 2 == 0:
-                    bias_by_r = bias_even[:, j // 2, BANK * half : BANK * (half + 1)].rearrange(
-                        "p (m r) -> p r m", m=M_BANK
-                    )
-                    nc.vector.tensor_tensor(out=switched, in0=by_r, in1=bias_by_r, op=ADD)
-                else:
-                    nc.scalar.copy(out=switched, in_=by_r)
+        def low_rows(j, half, y, r0, r1):
+            first = M_OUT * j + M_BANK * half
+            nc.vector.tensor_tensor(
+                out=out_sb[:, r0:r1, first : first + M_BANK],
+                in0=y[:].rearrange("p (m r) -> p r m", m=M_BANK)[:, r0:r1, :],
+                in1=bias_low[:, j, M_BANK * R_LOW * half : M_BANK * R_LOW * (half + 1)].rearrange(
+                    "p (m r) -> p r m", m=M_BANK
+                )[:, r0:r1, :],
+                op=ADD,
+            )
 
-        for c0 in range(0, R_HALF, R_CHUNK):
-            spread_odd = psum.tile([P, R_CHUNK, 2, R_HALF], BF16, name="spread_odd", tag="bank")
-            for i in range(R_CHUNK):
-                nc.tensor.transpose(
-                    out=spread_odd[:, i, :, :].rearrange("p rh w -> p (rh w)"),
-                    in_=b1_odd[:, c0 + i : c0 + i + 1].to_broadcast([P, P]),
-                    identity=ident_bf16[:],
-                )
-            for rh in range(2):
-                r0 = R_HALF * rh + c0
+        def high_rows(j, half, y):
+            first = M_OUT * j + M_BANK * half
+            nc.scalar.copy(
+                out=out_sb[:, R_LOW:R, first : first + M_BANK],
+                in_=y[:].rearrange("p (m r) -> p r m", m=M_BANK)[:, R_LOW:R, :],
+            )
+
+        def product(j, half):
+            y = psum.tile([P, BANK], F32, name="y", tag="bank")
+            nc.tensor.matmul_mx(
+                out=y[:],
+                lhsT=h_words[:, j, :].bitcast(FP8X4),
+                lhsT_scale=h_scales[:, j, :],
+                rhs=w_words[:, j, 2 * BANK * half : 2 * BANK * (half + 1)].bitcast(FP4X4),
+                rhs_scale=w_scales[:, j, BANK * half : BANK * (half + 1)],
+                start=True,
+                stop=True,
+            )
+            return y
+
+        for j in range(BLOCKS - 1):
+            for half in range(HALVES):
+                y = product(j, half)
+                low_rows(j, half, y, 0, R_LOW)
+                high_rows(j, half, y)
+
+        last = BLOCKS - 1
+        y_last = [product(last, half) for half in range(HALVES)]
+        for r0, r1 in ((0, R_FIRST), (R_FIRST, R_LOW)):
+            for half in range(HALVES):
+                low_rows(last, half, y_last[half], r0, r1)
+            nc.sync.dma_start(out=out[:, r0:r1, :], in_=out_sb[:, r0:r1, :])
+        for half in range(HALVES):
+            high_rows(last, half, y_last[half])
+
+        for s0 in range(R_LOW, R, R_STORE):
+            for r0 in range(s0, s0 + R_STORE, R_CHUNK):
+                spread_high = psum.tile([P, R_CHUNK, P], BF16, name="spread_high", tag="bank")
+                for i in range(R_CHUNK):
+                    c = r0 - R_LOW + i
+                    nc.tensor.transpose(
+                        out=spread_high[:, i, :], in_=b1_high[:, c : c + 1].to_broadcast([P, P]), identity=ident_bf16[:]
+                    )
                 rows = out_sb[:, r0 : r0 + R_CHUNK, :]
-                odd_columns = rows.rearrange("p r (j2 par m) -> p r j2 par m", par=2, m=M_OUT)[:, :, :, 1, :]
-                nc.vector.tensor_tensor(
-                    out=odd_columns,
-                    in0=spread_odd[:, :, rh, :].rearrange("p c (j2 m) -> p c j2 m", m=M_OUT),
-                    in1=odd_columns,
-                    op=ADD,
-                )
-                nc.sync.dma_start(out=out[:, r0 : r0 + R_CHUNK, :], in_=rows)
+                nc.vector.tensor_tensor(out=rows, in0=spread_high[:], in1=rows, op=ADD)
+            nc.sync.dma_start(out=out[:, s0 : s0 + R_STORE, :], in_=out_sb[:, s0 : s0 + R_STORE, :])

@@ -145,10 +145,10 @@ def tile_switchnet_fstar_pa_e_kernel(tc, x, k1_words, k1_scales, b1, out):
             first = M_OUT * j + M_BANK * half
             nc.vector.tensor_tensor(
                 out=out_sb[:, r0:r1, first : first + M_BANK],
-                in0=y[:].rearrange("p (m r) -> p r m", m=M_BANK)[:, r0:r1, :],
-                in1=bias_low[:, j, M_BANK * R_LOW * half : M_BANK * R_LOW * (half + 1)].rearrange(
+                in0=bias_low[:, j, M_BANK * R_LOW * half : M_BANK * R_LOW * (half + 1)].rearrange(
                     "p (m r) -> p r m", m=M_BANK
                 )[:, r0:r1, :],
+                in1=y[:].rearrange("p (m r) -> p r m", m=M_BANK)[:, r0:r1, :],
                 op=ADD,
             )
 

@@ -23,6 +23,7 @@ BANK = 512
 M_BANK = BANK // R
 HALVES = L // BANK
 R_LOW = R // 2
+R_VECTOR = 56
 R_FIRST = 16
 R_CHUNK = 8
 R_STORE = 32
@@ -48,7 +49,7 @@ def tile_switchnet_fstar_pa_e_kernel(tc, x, k1_words, k1_scales, b1, out):
         bias_low = keep.tile([P, BLOCKS, M_OUT * R_LOW], BF16)
         b1_four_rows = keep.tile([P, M_BANK * R_LOW], BF16)
         b1_words = keep.tile([P, P // M_BANK], F32)
-        b1_high = keep.tile([P, R - R_LOW], BF16)
+        b1_high = keep.tile([P, R - R_VECTOR], BF16)
 
         nc.vector.memset(w_scales[:].rearrange("p g n -> p (g n)").bitcast(I32), 0)
         nc.gpsimd.memset(b1_four_rows[P // 4 : P // 2, :], 0.0)
@@ -58,7 +59,7 @@ def tile_switchnet_fstar_pa_e_kernel(tc, x, k1_words, k1_scales, b1, out):
             out=b1_four_rows[0 : P // M_BANK, :].rearrange("p (q c) -> p q c", q=M_BANK),
             in_=b1.rearrange("o j (mh q rh c) -> o rh (j mh) q c", mh=HALVES, q=M_BANK, rh=2)[0, 0],
         )
-        nc.scalar.dma_start(out=b1_high[:], in_=b1.rearrange("o j (m rh c) -> o rh (j m) c", m=M_OUT, rh=2)[0, 1])
+        nc.scalar.dma_start(out=b1_high[:], in_=b1.rearrange("o j (m r) -> (o j m) r", m=M_OUT)[:, R_VECTOR:R])
 
         x_flat = x.rearrange("b g c -> b (g c)")
         x_rows = []
@@ -155,8 +156,8 @@ def tile_switchnet_fstar_pa_e_kernel(tc, x, k1_words, k1_scales, b1, out):
         def high_rows(j, half, y):
             first = M_OUT * j + M_BANK * half
             nc.scalar.copy(
-                out=out_sb[:, R_LOW:R, first : first + M_BANK],
-                in_=y[:].rearrange("p (m r) -> p r m", m=M_BANK)[:, R_LOW:R, :],
+                out=out_sb[:, R_VECTOR:R, first : first + M_BANK],
+                in_=y[:].rearrange("p (m r) -> p r m", m=M_BANK)[:, R_VECTOR:R, :],
             )
 
         def product(j, half):
@@ -175,26 +176,26 @@ def tile_switchnet_fstar_pa_e_kernel(tc, x, k1_words, k1_scales, b1, out):
         for j in range(BLOCKS - 1):
             for half in range(HALVES):
                 y = product(j, half)
-                low_rows(j, half, y, 0, R_LOW)
+                low_rows(j, half, y, 0, R_VECTOR)
                 high_rows(j, half, y)
 
         last = BLOCKS - 1
         y_last = [product(last, half) for half in range(HALVES)]
-        for r0, r1 in ((0, R_FIRST), (R_FIRST, R_LOW)):
+        for r0, r1 in ((0, R_FIRST), (R_FIRST, R_VECTOR)):
             for half in range(HALVES):
                 low_rows(last, half, y_last[half], r0, r1)
             nc.sync.dma_start(out=out[:, r0:r1, :], in_=out_sb[:, r0:r1, :])
         for half in range(HALVES):
             high_rows(last, half, y_last[half])
 
-        for s0 in range(R_LOW, R, R_STORE):
-            for r0 in range(s0, s0 + R_STORE, R_CHUNK):
+        for s0, s1 in ((R_VECTOR, R_VECTOR + R_STORE), (R_VECTOR + R_STORE, R)):
+            for r0 in range(s0, s1, R_CHUNK):
                 spread_high = psum.tile([P, R_CHUNK, P], BF16, name="spread_high", tag="bank")
                 for i in range(R_CHUNK):
-                    c = r0 - R_LOW + i
+                    c = r0 - R_VECTOR + i
                     nc.tensor.transpose(
                         out=spread_high[:, i, :], in_=b1_high[:, c : c + 1].to_broadcast([P, P]), identity=ident_bf16[:]
                     )
                 rows = out_sb[:, r0 : r0 + R_CHUNK, :]
                 nc.vector.tensor_tensor(out=rows, in0=spread_high[:], in1=rows, op=ADD)
-            nc.sync.dma_start(out=out[:, s0 : s0 + R_STORE, :], in_=out_sb[:, s0 : s0 + R_STORE, :])
+            nc.sync.dma_start(out=out[:, s0:s1, :], in_=out_sb[:, s0:s1, :])

@@ -82,8 +82,13 @@ def tile_switchnet_fstar_pa_e_kernel(tc, x, k1_words, k1_scales, b1, out):
                 )
 
         words_i32 = k1_words.bitcast(I32)
-        for j in range(BLOCKS):
+        for j in range(BLOCKS - 1):
             nc.sync.dma_start(out=w_words[:, j, :].bitcast(I32), in_=words_i32[j])
+        for half in range(HALVES):
+            nc.sync.dma_start(
+                out=w_words[:, BLOCKS - 1, 2 * BANK * half : 2 * BANK * (half + 1)].bitcast(I32),
+                in_=words_i32[BLOCKS - 1][:, BANK // 2 * half : BANK // 2 * (half + 1)],
+            )
 
         def gather_windows(br):
             windows = stage.tile([P, GRID, SIDE, ROW], BF16, name="windows")
@@ -181,9 +186,9 @@ def tile_switchnet_fstar_pa_e_kernel(tc, x, k1_words, k1_scales, b1, out):
 
         last = BLOCKS - 1
         y_last = [product(last, half) for half in range(HALVES)]
+        low_rows(last, 0, y_last[0], 0, R_VECTOR)
         for r0, r1 in ((0, R_FIRST), (R_FIRST, R_VECTOR)):
-            for half in range(HALVES):
-                low_rows(last, half, y_last[half], r0, r1)
+            low_rows(last, 1, y_last[1], r0, r1)
             nc.sync.dma_start(out=out[:, r0:r1, :], in_=out_sb[:, r0:r1, :])
         for half in range(HALVES):
             high_rows(last, half, y_last[half])

@@ -22,11 +22,10 @@ L = M_OUT * R
 BANK = 512
 M_BANK = BANK // R
 HALVES = L // BANK
-R_LOW = R // 2
-R_VECTOR = 56
-R_FIRST = 16
 R_CHUNK = 8
-R_STORE = 32
+R_LOW = 24
+R_TOP = 104
+FUSED_BLOCKS = 2
 
 FLOPS = 2 * P * K * L * BLOCKS
 
@@ -46,20 +45,13 @@ def tile_switchnet_fstar_pa_e_kernel(tc, x, k1_words, k1_scales, b1, out):
         h_words = keep.tile([P, BLOCKS, P], U32, align_bytes=64)
         h_scales = keep.tile([P, BLOCKS, P], U8, align_bytes=64)
         out_sb = keep.tile([P, R, BLOCKS * M_OUT], F32)
-        bias_low = keep.tile([P, BLOCKS, M_OUT * R_LOW], BF16)
-        b1_four_rows = keep.tile([P, M_BANK * R_LOW], BF16)
-        b1_words = keep.tile([P, P // M_BANK], F32)
-        b1_high = keep.tile([P, R - R_VECTOR], BF16)
+        b1_cols = keep.tile([P, R], BF16)
+        bias_low = keep.tile([P, R_LOW, P], BF16)
+        bias_top = keep.tile([P, R - R_TOP, P], BF16)
 
         nc.vector.memset(w_scales[:].rearrange("p g n -> p (g n)").bitcast(I32), 0)
-        nc.gpsimd.memset(b1_four_rows[P // 4 : P // 2, :], 0.0)
-        nc.gpsimd.memset(b1_four_rows[P // 2 : P, :], 0.0)
 
-        nc.scalar.dma_start(
-            out=b1_four_rows[0 : P // M_BANK, :].rearrange("p (q c) -> p q c", q=M_BANK),
-            in_=b1.rearrange("o j (mh q rh c) -> o rh (j mh) q c", mh=HALVES, q=M_BANK, rh=2)[0, 0],
-        )
-        nc.scalar.dma_start(out=b1_high[:], in_=b1.rearrange("o j (m r) -> (o j m) r", m=M_OUT)[:, R_VECTOR:R])
+        nc.scalar.dma_start(out=b1_cols[:], in_=b1.rearrange("o j (m r) -> (o j m) r", m=M_OUT))
 
         x_flat = x.rearrange("b g c -> b (g c)")
         x_rows = []
@@ -116,53 +108,30 @@ def tile_switchnet_fstar_pa_e_kernel(tc, x, k1_words, k1_scales, b1, out):
                 )
             return grouped
 
-        def spread_low_bias(j):
-            spread = psum.tile([P, M_BANK, P], F32, name="spread", tag="bank")
-            for i in range(M_BANK):
-                col = HALVES * j + i
+        def spread_bias(r0):
+            spread = psum.tile([P, R_CHUNK, P], BF16, name="spread", tag="bank")
+            for i in range(R_CHUNK):
                 nc.tensor.transpose(
-                    out=spread[:, i, :], in_=b1_words[:, col : col + 1].to_broadcast([P, P]), identity=ident_f32[:]
+                    out=spread[:, i, :],
+                    in_=b1_cols[:, r0 + i : r0 + i + 1].to_broadcast([P, P]),
+                    identity=ident_bf16[:],
                 )
-            nc.scalar.copy(
-                out=bias_low[:, j : j + 2, :].rearrange("p j w -> p (j w)").bitcast(F32),
-                in_=spread[:].rearrange("p i w -> p (i w)"),
-            )
-
-        b1_t = psum.tile([P, P], F32, name="b1_t", tag="bank")
-        nc.tensor.transpose(out=b1_t[:], in_=b1_four_rows[:].bitcast(F32), identity=ident_f32[:])
-        nc.scalar.copy(out=b1_words[:], in_=b1_t[:, 0 : P // M_BANK])
+            return spread
 
         windows_next = gather_windows(0)
         for br in range(GRID):
             windows = windows_next
             if br + 1 < GRID:
                 windows_next = gather_windows(br + 1)
-            spread_low_bias(GRID * br)
-            spread_low_bias(GRID * br + 2)
+            r0 = br * R_CHUNK
+            if r0 < R_LOW:
+                nc.scalar.copy(out=bias_low[:, r0 : r0 + R_CHUNK, :], in_=spread_bias(r0)[:])
             grouped = transpose_windows(windows)
             blocks = slice(br * GRID, (br + 1) * GRID)
             nc.vector.quantize_mx(
                 out=h_words[:, blocks, :].rearrange("p j b -> p (j b)").bitcast(FP8X4),
                 scales=h_scales[:, blocks, :].rearrange("p j b -> p (j b)"),
                 in_=grouped[:].rearrange("p c b t -> p (c b t)"),
-            )
-
-        def low_rows(j, half, y, r0, r1):
-            first = M_OUT * j + M_BANK * half
-            nc.vector.tensor_tensor(
-                out=out_sb[:, r0:r1, first : first + M_BANK],
-                in0=bias_low[:, j, M_BANK * R_LOW * half : M_BANK * R_LOW * (half + 1)].rearrange(
-                    "p (m r) -> p r m", m=M_BANK
-                )[:, r0:r1, :],
-                in1=y[:].rearrange("p (m r) -> p r m", m=M_BANK)[:, r0:r1, :],
-                op=ADD,
-            )
-
-        def high_rows(j, half, y):
-            first = M_OUT * j + M_BANK * half
-            nc.scalar.copy(
-                out=out_sb[:, R_VECTOR:R, first : first + M_BANK],
-                in_=y[:].rearrange("p (m r) -> p r m", m=M_BANK)[:, R_VECTOR:R, :],
             )
 
         def product(j, half):
@@ -176,31 +145,66 @@ def tile_switchnet_fstar_pa_e_kernel(tc, x, k1_words, k1_scales, b1, out):
                 start=True,
                 stop=True,
             )
-            return y
+            return y[:].rearrange("p (m r) -> p r m", m=M_BANK)
 
-        for j in range(BLOCKS - 1):
-            for half in range(HALVES):
-                y = product(j, half)
-                low_rows(j, half, y, 0, R_VECTOR)
-                high_rows(j, half, y)
+        def columns(j, half):
+            first = M_OUT * j + M_BANK * half
+            return slice(first, first + M_BANK)
+
+        for j in range(BLOCKS - FUSED_BLOCKS):
+            nc.vector.tensor_copy(out=out_sb[:, :, columns(j, 0)], in_=product(j, 0))
+            nc.scalar.copy(out=out_sb[:, :, columns(j, 1)], in_=product(j, 1))
+            if j % 2 == 1:
+                pair = slice(M_OUT * (j - 1), M_OUT * (j + 1))
+                rows = out_sb[:, 0:R_LOW, pair]
+                nc.gpsimd.tensor_tensor(out=rows, in0=rows, in1=bias_low[:, :, pair], op=ADD)
+
+        def low_rows(y, j, half):
+            nc.vector.tensor_tensor(
+                out=out_sb[:, 0:R_LOW, columns(j, half)],
+                in0=bias_low[:, :, columns(j, half)],
+                in1=y[:, 0:R_LOW, :],
+                op=ADD,
+            )
+
+        def high_rows(y, j, half):
+            copy = nc.scalar.copy if half else nc.vector.tensor_copy
+            copy(out=out_sb[:, R_LOW:R, columns(j, half)], in_=y[:, R_LOW:R, :])
 
         last = BLOCKS - 1
+        for j in range(BLOCKS - FUSED_BLOCKS, last):
+            for half in range(HALVES):
+                y = product(j, half)
+                low_rows(y, j, half)
+                high_rows(y, j, half)
         y_last = [product(last, half) for half in range(HALVES)]
-        low_rows(last, 0, y_last[0], 0, R_VECTOR)
-        for r0, r1 in ((0, R_FIRST), (R_FIRST, R_VECTOR)):
-            low_rows(last, 1, y_last[1], r0, r1)
-            nc.sync.dma_start(out=out[:, r0:r1, :], in_=out_sb[:, r0:r1, :])
         for half in range(HALVES):
-            high_rows(last, half, y_last[half])
+            low_rows(y_last[half], last, half)
+        nc.sync.dma_start(out=out[:, 0:R_LOW, :], in_=out_sb[:, 0:R_LOW, :])
+        for half in range(HALVES):
+            high_rows(y_last[half], last, half)
 
-        for s0, s1 in ((R_VECTOR, R_VECTOR + R_STORE), (R_VECTOR + R_STORE, R)):
-            for r0 in range(s0, s1, R_CHUNK):
-                spread_high = psum.tile([P, R_CHUNK, P], BF16, name="spread_high", tag="bank")
-                for i in range(R_CHUNK):
-                    c = r0 - R_VECTOR + i
-                    nc.tensor.transpose(
-                        out=spread_high[:, i, :], in_=b1_high[:, c : c + 1].to_broadcast([P, P]), identity=ident_bf16[:]
-                    )
-                rows = out_sb[:, r0 : r0 + R_CHUNK, :]
-                nc.vector.tensor_tensor(out=rows, in0=spread_high[:], in1=rows, op=ADD)
-            nc.sync.dma_start(out=out[:, s0:s1, :], in_=out_sb[:, s0:s1, :])
+        def vector_rows(r0):
+            rows = out_sb[:, r0 : r0 + R_CHUNK, :]
+            nc.vector.tensor_tensor(out=rows, in0=spread_bias(r0)[:], in1=rows, op=ADD)
+
+        def gpsimd_rows(r0):
+            rows = out_sb[:, r0 : r0 + R_CHUNK, :]
+            bias = bias_top[:, r0 - R_TOP : r0 - R_TOP + R_CHUNK, :]
+            nc.scalar.copy(out=bias, in_=spread_bias(r0)[:])
+            nc.gpsimd.tensor_tensor(out=rows, in0=rows, in1=bias, op=ADD)
+
+        def store(r0, r1):
+            nc.sync.dma_start(out=out[:, r0:r1, :], in_=out_sb[:, r0:r1, :])
+
+        for i, r0 in enumerate(range(R_LOW, R_TOP, R_CHUNK)):
+            vector_rows(r0)
+            if R_TOP + i * R_CHUNK < R:
+                gpsimd_rows(R_TOP + i * R_CHUNK)
+            if i == 0:
+                store(r0, r0 + R_CHUNK)
+            elif i % 2 == 0:
+                store(r0 - R_CHUNK, r0 + R_CHUNK)
+            if i == 6:
+                store(R_TOP, R)
+        store(R_TOP - R_CHUNK, R_TOP)

@@ -23,8 +23,8 @@ BANK = 512
 M_BANK = BANK // R
 HALVES = L // BANK
 R_CHUNK = 8
-R_LOW = 24
-R_TOP = 104
+R_LOW = 16
+R_TOP = 96
 FUSED_BLOCKS = 2
 
 FLOPS = 2 * P * K * L * BLOCKS
@@ -118,14 +118,13 @@ def tile_switchnet_fstar_pa_e_kernel(tc, x, k1_words, k1_scales, b1, out):
                 )
             return spread
 
+        for r0 in range(0, R_LOW, R_CHUNK):
+            nc.scalar.copy(out=bias_low[:, r0 : r0 + R_CHUNK, :], in_=spread_bias(r0)[:])
         windows_next = gather_windows(0)
         for br in range(GRID):
             windows = windows_next
             if br + 1 < GRID:
                 windows_next = gather_windows(br + 1)
-            r0 = br * R_CHUNK
-            if r0 < R_LOW:
-                nc.scalar.copy(out=bias_low[:, r0 : r0 + R_CHUNK, :], in_=spread_bias(r0)[:])
             grouped = transpose_windows(windows)
             blocks = slice(br * GRID, (br + 1) * GRID)
             nc.vector.quantize_mx(
@@ -154,10 +153,11 @@ def tile_switchnet_fstar_pa_e_kernel(tc, x, k1_words, k1_scales, b1, out):
         for j in range(BLOCKS - FUSED_BLOCKS):
             nc.vector.tensor_copy(out=out_sb[:, :, columns(j, 0)], in_=product(j, 0))
             nc.scalar.copy(out=out_sb[:, :, columns(j, 1)], in_=product(j, 1))
-            if j % 2 == 1:
-                pair = slice(M_OUT * (j - 1), M_OUT * (j + 1))
-                rows = out_sb[:, 0:R_LOW, pair]
-                nc.gpsimd.tensor_tensor(out=rows, in0=rows, in1=bias_low[:, :, pair], op=ADD)
+            single = j >= BLOCKS - 2 * FUSED_BLOCKS
+            if single or j % 2 == 1:
+                drained = slice(M_OUT * (j if single else j - 1), M_OUT * (j + 1))
+                rows = out_sb[:, 0:R_LOW, drained]
+                nc.gpsimd.tensor_tensor(out=rows, in0=rows, in1=bias_low[:, :, drained], op=ADD)
 
         def low_rows(y, j, half):
             nc.vector.tensor_tensor(
@@ -167,22 +167,25 @@ def tile_switchnet_fstar_pa_e_kernel(tc, x, k1_words, k1_scales, b1, out):
                 op=ADD,
             )
 
-        def high_rows(y, j, half):
-            copy = nc.scalar.copy if half else nc.vector.tensor_copy
-            copy(out=out_sb[:, R_LOW:R, columns(j, half)], in_=y[:, R_LOW:R, :])
+        def high_rows(copy, y, j, half, r0, r1):
+            copy(out=out_sb[:, r0:r1, columns(j, half)], in_=y[:, r0:r1, :])
+
+        def store(r0, r1):
+            nc.sync.dma_start(out=out[:, r0:r1, :], in_=out_sb[:, r0:r1, :])
 
         last = BLOCKS - 1
         for j in range(BLOCKS - FUSED_BLOCKS, last):
             for half in range(HALVES):
                 y = product(j, half)
                 low_rows(y, j, half)
-                high_rows(y, j, half)
+                high_rows(nc.scalar.copy if half else nc.vector.tensor_copy, y, j, half, R_LOW, R)
         y_last = [product(last, half) for half in range(HALVES)]
         for half in range(HALVES):
             low_rows(y_last[half], last, half)
-        nc.sync.dma_start(out=out[:, 0:R_LOW, :], in_=out_sb[:, 0:R_LOW, :])
-        for half in range(HALVES):
-            high_rows(y_last[half], last, half)
+        store(0, R_LOW)
+        high_rows(nc.scalar.copy, y_last[0], last, 0, R_LOW, R)
+        for r0, r1 in ((R_LOW, R_LOW + 2 * R_CHUNK), (R_LOW + 2 * R_CHUNK, R)):
+            high_rows(nc.scalar.copy, y_last[1], last, 1, r0, r1)
 
         def vector_rows(r0):
             rows = out_sb[:, r0 : r0 + R_CHUNK, :]
@@ -194,17 +197,15 @@ def tile_switchnet_fstar_pa_e_kernel(tc, x, k1_words, k1_scales, b1, out):
             nc.scalar.copy(out=bias, in_=spread_bias(r0)[:])
             nc.gpsimd.tensor_tensor(out=rows, in0=rows, in1=bias, op=ADD)
 
-        def store(r0, r1):
-            nc.sync.dma_start(out=out[:, r0:r1, :], in_=out_sb[:, r0:r1, :])
-
+        stored = R_LOW
         for i, r0 in enumerate(range(R_LOW, R_TOP, R_CHUNK)):
             vector_rows(r0)
             if R_TOP + i * R_CHUNK < R:
                 gpsimd_rows(R_TOP + i * R_CHUNK)
-            if i == 0:
-                store(r0, r0 + R_CHUNK)
-            elif i % 2 == 0:
-                store(r0 - R_CHUNK, r0 + R_CHUNK)
-            if i == 6:
-                store(R_TOP, R)
-        store(R_TOP - R_CHUNK, R_TOP)
+            if i < 5 or i % 2 == 0 or r0 + R_CHUNK == R_TOP:
+                store(stored, r0 + R_CHUNK)
+                stored = r0 + R_CHUNK
+            if i == 4:
+                store(R_TOP, R_TOP + 2 * R_CHUNK)
+            if i == 8:
+                store(R_TOP + 2 * R_CHUNK, R)

@@ -23,8 +23,8 @@ BANK = 512
 M_BANK = BANK // R
 HALVES = L // BANK
 R_CHUNK = 8
-R_LOW = 16
-R_TOP = 96
+R_LOW = 24
+R_TOP = 104
 FUSED_BLOCKS = 2
 
 FLOPS = 2 * P * K * L * BLOCKS
@@ -37,8 +37,6 @@ def tile_switchnet_fstar_pa_e_kernel(tc, x, k1_words, k1_scales, b1, out):
     ) as psum, tc.manual_schedule():
         ident_f32 = keep.tile([P, P], F32)
         make_identity(nc, ident_f32[:])
-        ident_bf16 = keep.tile([P, P], BF16)
-        make_identity(nc, ident_bf16[:])
 
         w_words = keep.tile([P, BLOCKS, 2 * L], U8, align_bytes=64)
         w_scales = keep.tile([P, BLOCKS, L], U8, align_bytes=64)
@@ -46,8 +44,8 @@ def tile_switchnet_fstar_pa_e_kernel(tc, x, k1_words, k1_scales, b1, out):
         h_scales = keep.tile([P, BLOCKS, P], U8, align_bytes=64)
         out_sb = keep.tile([P, R, BLOCKS * M_OUT], F32)
         b1_cols = keep.tile([P, R], BF16)
-        bias_low = keep.tile([P, R_LOW, P], BF16)
-        bias_top = keep.tile([P, R - R_TOP, P], BF16)
+        bias_low = keep.tile([P, R_LOW // 2, P], F32)
+        bias_top = keep.tile([P, (R - R_TOP) // 2, P], F32)
 
         nc.vector.memset(w_scales[:].rearrange("p g n -> p (g n)").bitcast(I32), 0)
 
@@ -109,17 +107,23 @@ def tile_switchnet_fstar_pa_e_kernel(tc, x, k1_words, k1_scales, b1, out):
             return grouped
 
         def spread_bias(r0):
-            spread = psum.tile([P, R_CHUNK, P], BF16, name="spread", tag="bank")
-            for i in range(R_CHUNK):
+            words = b1_cols[:].bitcast(F32)
+            spread = psum.tile([P, R_CHUNK // 2, P], F32, name="spread", tag="bank")
+            for i in range(R_CHUNK // 2):
+                col = r0 // 2 + i
                 nc.tensor.transpose(
-                    out=spread[:, i, :],
-                    in_=b1_cols[:, r0 + i : r0 + i + 1].to_broadcast([P, P]),
-                    identity=ident_bf16[:],
+                    out=spread[:, i, :], in_=words[:, col : col + 1].to_broadcast([P, P]), identity=ident_f32[:]
                 )
             return spread
 
+        def by_pairs(rows):
+            return rows.rearrange("p (i e) n -> p i e n", e=2)
+
+        def bias_rows(words):
+            return words.bitcast(BF16).rearrange("p i (n e) -> p i e n", e=2)
+
         for r0 in range(0, R_LOW, R_CHUNK):
-            nc.scalar.copy(out=bias_low[:, r0 : r0 + R_CHUNK, :], in_=spread_bias(r0)[:])
+            nc.scalar.copy(out=bias_low[:, r0 // 2 : (r0 + R_CHUNK) // 2, :], in_=spread_bias(r0)[:])
         windows_next = gather_windows(0)
         for br in range(GRID):
             windows = windows_next
@@ -156,14 +160,14 @@ def tile_switchnet_fstar_pa_e_kernel(tc, x, k1_words, k1_scales, b1, out):
             single = j >= BLOCKS - 2 * FUSED_BLOCKS
             if single or j % 2 == 1:
                 drained = slice(M_OUT * (j if single else j - 1), M_OUT * (j + 1))
-                rows = out_sb[:, 0:R_LOW, drained]
-                nc.gpsimd.tensor_tensor(out=rows, in0=rows, in1=bias_low[:, :, drained], op=ADD)
+                rows = by_pairs(out_sb[:, 0:R_LOW, drained])
+                nc.gpsimd.tensor_tensor(out=rows, in0=rows, in1=bias_rows(bias_low[:])[:, :, :, drained], op=ADD)
 
         def low_rows(y, j, half):
             nc.vector.tensor_tensor(
-                out=out_sb[:, 0:R_LOW, columns(j, half)],
-                in0=bias_low[:, :, columns(j, half)],
-                in1=y[:, 0:R_LOW, :],
+                out=by_pairs(out_sb[:, 0:R_LOW, columns(j, half)]),
+                in0=bias_rows(bias_low[:])[:, :, :, columns(j, half)],
+                in1=by_pairs(y[:, 0:R_LOW, :]),
                 op=ADD,
             )
 
@@ -188,24 +192,27 @@ def tile_switchnet_fstar_pa_e_kernel(tc, x, k1_words, k1_scales, b1, out):
             high_rows(nc.scalar.copy, y_last[1], last, 1, r0, r1)
 
         def vector_rows(r0):
-            rows = out_sb[:, r0 : r0 + R_CHUNK, :]
-            nc.vector.tensor_tensor(out=rows, in0=spread_bias(r0)[:], in1=rows, op=ADD)
+            rows = by_pairs(out_sb[:, r0 : r0 + R_CHUNK, :])
+            nc.vector.tensor_tensor(out=rows, in0=bias_rows(spread_bias(r0)[:]), in1=rows, op=ADD)
 
         def gpsimd_rows(r0):
-            rows = out_sb[:, r0 : r0 + R_CHUNK, :]
-            bias = bias_top[:, r0 - R_TOP : r0 - R_TOP + R_CHUNK, :]
+            rows = by_pairs(out_sb[:, r0 : r0 + R_CHUNK, :])
+            bias = bias_top[:, (r0 - R_TOP) // 2 : (r0 - R_TOP + R_CHUNK) // 2, :]
             nc.scalar.copy(out=bias, in_=spread_bias(r0)[:])
-            nc.gpsimd.tensor_tensor(out=rows, in0=rows, in1=bias, op=ADD)
+            nc.gpsimd.tensor_tensor(out=rows, in0=rows, in1=bias_rows(bias), op=ADD)
 
-        stored = R_LOW
-        for i, r0 in enumerate(range(R_LOW, R_TOP, R_CHUNK)):
-            vector_rows(r0)
-            if R_TOP + i * R_CHUNK < R:
-                gpsimd_rows(R_TOP + i * R_CHUNK)
-            if i < 5 or i % 2 == 0 or r0 + R_CHUNK == R_TOP:
-                store(stored, r0 + R_CHUNK)
-                stored = r0 + R_CHUNK
-            if i == 4:
-                store(R_TOP, R_TOP + 2 * R_CHUNK)
-            if i == 8:
-                store(R_TOP + 2 * R_CHUNK, R)
+        top = R - 2 * R_CHUNK
+        for chunks, stored in (
+            ((24,), (24, 32)),
+            ((32, top, 40), (32, 48)),
+            ((top + R_CHUNK, 48, 56), (48, 64)),
+            ((R_TOP,), (top, R)),
+            ((64, 72), (64, 80)),
+            ((80, 88, 96), (80, top)),
+        ):
+            for r0 in chunks:
+                if r0 < R_TOP:
+                    vector_rows(r0)
+                else:
+                    gpsimd_rows(r0)
+            store(stored[0], stored[1])

import concourse.mybir as mybir
from concourse.masks import make_identity

F32 = mybir.dt.float32
BF16 = mybir.dt.bfloat16
I32 = mybir.dt.int32
U32 = mybir.dt.uint32
U8 = mybir.dt.uint8
FP8X4 = mybir.dt.float8_e4m3fn_x4
FP4X4 = mybir.dt.float4_e2m1fn_x4
ADD = mybir.AluOpType.add

P = 128
GRID = 4
SIDE = 16
ROW = 32
BLOCKS = GRID * GRID
K = SIDE * ROW
R = 128
M_OUT = 8
L = M_OUT * R
BANK = 512
M_BANK = BANK // R
HALVES = L // BANK
R_CHUNK = 8
R_LOW = 24
R_TOP = 104
FUSED_BLOCKS = 2

FLOPS = 2 * P * K * L * BLOCKS


def tile_switchnet_fstar_pa_e_kernel(tc, x, k1_words, k1_scales, b1, out):
    nc = tc.nc
    with tc.tile_pool(name="keep", bufs=1) as keep, tc.tile_pool(name="stage", bufs=2) as stage, tc.psum_pool(
        name="psum", bufs=8
    ) as psum, tc.manual_schedule():
        ident_f32 = keep.tile([P, P], F32)
        make_identity(nc, ident_f32[:])

        w_words = keep.tile([P, BLOCKS, 2 * L], U8, align_bytes=64)
        w_scales = keep.tile([P, BLOCKS, L], U8, align_bytes=64)
        h_words = keep.tile([P, BLOCKS, P], U32, align_bytes=64)
        h_scales = keep.tile([P, BLOCKS, P], U8, align_bytes=64)
        out_sb = keep.tile([P, R, BLOCKS * M_OUT], F32)
        b1_cols = keep.tile([P, R], BF16)
        bias_low = keep.tile([P, R_LOW // 2, P], F32)
        bias_top = keep.tile([P, (R - R_TOP) // 2, P], F32)

        nc.vector.memset(w_scales[:].rearrange("p g n -> p (g n)").bitcast(I32), 0)

        nc.scalar.dma_start(out=b1_cols[:], in_=b1.rearrange("o j (m r) -> (o j m) r", m=M_OUT))

        x_flat = x.rearrange("b g c -> b (g c)")
        x_rows = []
        for br in range(GRID):
            x_raw = keep.tile([P, SIDE, GRID, ROW], BF16, name="x_raw%d" % br)
            nc.sync.dma_start(
                out=x_raw[:].rearrange("p r c k -> p (r c k)"),
                in_=x_flat[:, br * GRID * K : (br + 1) * GRID * K],
            )
            x_rows.append(x_raw)

        scales_i32 = k1_scales.bitcast(I32)
        for g0 in range(0, BLOCKS, BLOCKS // 2):
            g1 = g0 + BLOCKS // 2
            for q in range(8):
                first = 32 * (q // 4) + q % 4
                nc.sync.dma_start(
                    out=w_scales[first:P:64, g0:g1, :].bitcast(I32),
                    in_=scales_i32[g0:g1, q:16:8, :].rearrange("g h n -> h g n"),
                )

        words_i32 = k1_words.bitcast(I32)
        for j in range(BLOCKS - 1):
            nc.sync.dma_start(out=w_words[:, j, :].bitcast(I32), in_=words_i32[j])
        for half in range(HALVES):
            nc.sync.dma_start(
                out=w_words[:, BLOCKS - 1, 2 * BANK * half : 2 * BANK * (half + 1)].bitcast(I32),
                in_=words_i32[BLOCKS - 1][:, BANK // 2 * half : BANK // 2 * (half + 1)],
            )

        def gather_windows(br):
            windows = stage.tile([P, GRID, SIDE, ROW], BF16, name="windows")
            nc.vector.tensor_copy(out=windows[:], in_=x_rows[br][:].rearrange("p r c k -> p c r k"))
            return windows

        def transpose_windows(windows):
            pairs = windows[:].rearrange("p c r k -> p (c r k)").bitcast(F32)
            grouped = stage.tile([P, GRID, P, 4], BF16, align_bytes=64, name="grouped")
            for c0 in range(0, GRID, 2):
                xt = psum.tile([P, 2, 2, P], F32, name="xt", tag="bank")
                for c in range(2):
                    for u in range(2):
                        nc.tensor.transpose(
                            out=xt[:, c, u, :],
                            in_=pairs[:, (c0 + c) * (K // 2) + u : (c0 + c + 1) * (K // 2) : 2],
                            identity=ident_f32[:],
                        )
                nc.scalar.copy(
                    out=grouped[:, c0 : c0 + 2, :, :]
                    .rearrange("p c b t -> p (c b t)")
                    .bitcast(F32)
                    .rearrange("p (c b u) -> p c b u", c=2, u=2),
                    in_=xt[:].rearrange("p c u b -> p c b u"),
                )
            return grouped

        def spread_bias(r0):
            words = b1_cols[:].bitcast(F32)
            spread = psum.tile([P, R_CHUNK // 2, P], F32, name="spread", tag="bank")
            for i in range(R_CHUNK // 2):
                col = r0 // 2 + i
                nc.tensor.transpose(
                    out=spread[:, i, :], in_=words[:, col : col + 1].to_broadcast([P, P]), identity=ident_f32[:]
                )
            return spread

        def by_pairs(rows):
            return rows.rearrange("p (i e) n -> p i e n", e=2)

        def bias_rows(words):
            return words.bitcast(BF16).rearrange("p i (n e) -> p i e n", e=2)

        for r0 in range(0, R_LOW, R_CHUNK):
            nc.scalar.copy(out=bias_low[:, r0 // 2 : (r0 + R_CHUNK) // 2, :], in_=spread_bias(r0)[:])
        windows_next = gather_windows(0)
        for br in range(GRID):
            windows = windows_next
            if br + 1 < GRID:
                windows_next = gather_windows(br + 1)
            grouped = transpose_windows(windows)
            blocks = slice(br * GRID, (br + 1) * GRID)
            nc.vector.quantize_mx(
                out=h_words[:, blocks, :].rearrange("p j b -> p (j b)").bitcast(FP8X4),
                scales=h_scales[:, blocks, :].rearrange("p j b -> p (j b)"),
                in_=grouped[:].rearrange("p c b t -> p (c b t)"),
            )

        def product(j, half):
            y = psum.tile([P, BANK], F32, name="y", tag="bank")
            nc.tensor.matmul_mx(
                out=y[:],
                lhsT=h_words[:, j, :].bitcast(FP8X4),
                lhsT_scale=h_scales[:, j, :],
                rhs=w_words[:, j, 2 * BANK * half : 2 * BANK * (half + 1)].bitcast(FP4X4),
                rhs_scale=w_scales[:, j, BANK * half : BANK * (half + 1)],
                start=True,
                stop=True,
            )
            return y[:].rearrange("p (m r) -> p r m", m=M_BANK)

        def columns(j, half):
            first = M_OUT * j + M_BANK * half
            return slice(first, first + M_BANK)

        for j in range(BLOCKS - FUSED_BLOCKS):
            nc.vector.tensor_copy(out=out_sb[:, :, columns(j, 0)], in_=product(j, 0))
            nc.scalar.copy(out=out_sb[:, :, columns(j, 1)], in_=product(j, 1))
            single = j >= BLOCKS - 2 * FUSED_BLOCKS
            if single or j % 2 == 1:
                drained = slice(M_OUT * (j if single else j - 1), M_OUT * (j + 1))
                rows = by_pairs(out_sb[:, 0:R_LOW, drained])
                nc.gpsimd.tensor_tensor(out=rows, in0=rows, in1=bias_rows(bias_low[:])[:, :, :, drained], op=ADD)

        def low_rows(y, j, half):
            nc.vector.tensor_tensor(
                out=by_pairs(out_sb[:, 0:R_LOW, columns(j, half)]),
                in0=bias_rows(bias_low[:])[:, :, :, columns(j, half)],
                in1=by_pairs(y[:, 0:R_LOW, :]),
                op=ADD,
            )

        def high_rows(copy, y, j, half, r0, r1):
            copy(out=out_sb[:, r0:r1, columns(j, half)], in_=y[:, r0:r1, :])

        def store(r0, r1):
            nc.sync.dma_start(out=out[:, r0:r1, :], in_=out_sb[:, r0:r1, :])

        last = BLOCKS - 1
        for j in range(BLOCKS - FUSED_BLOCKS, last):
            for half in range(HALVES):
                y = product(j, half)
                low_rows(y, j, half)
                high_rows(nc.scalar.copy if half else nc.vector.tensor_copy, y, j, half, R_LOW, R)
        y_last = [product(last, half) for half in range(HALVES)]
        for half in range(HALVES):
            low_rows(y_last[half], last, half)
        store(0, R_LOW)
        high_rows(nc.scalar.copy, y_last[0], last, 0, R_LOW, R)
        for r0, r1 in ((R_LOW, R_LOW + 2 * R_CHUNK), (R_LOW + 2 * R_CHUNK, R)):
            high_rows(nc.scalar.copy, y_last[1], last, 1, r0, r1)

        def vector_rows(r0):
            rows = by_pairs(out_sb[:, r0 : r0 + R_CHUNK, :])
            nc.vector.tensor_tensor(out=rows, in0=bias_rows(spread_bias(r0)[:]), in1=rows, op=ADD)

        def gpsimd_rows(r0):
            rows = by_pairs(out_sb[:, r0 : r0 + R_CHUNK, :])
            bias = bias_top[:, (r0 - R_TOP) // 2 : (r0 - R_TOP + R_CHUNK) // 2, :]
            nc.scalar.copy(out=bias, in_=spread_bias(r0)[:])
            nc.gpsimd.tensor_tensor(out=rows, in0=rows, in1=bias_rows(bias), op=ADD)

        top = R - 2 * R_CHUNK
        for chunks, stored in (
            ((24,), (24, 32)),
            ((32, top, 40), (32, 48)),
            ((top + R_CHUNK, 48, 56), (48, 64)),
            ((R_TOP,), (top, R)),
            ((64, 72), (64, 80)),
            ((80, 88, 96), (80, top)),
        ):
            for r0 in chunks:
                if r0 < R_TOP:
                    vector_rows(r0)
                else:
                    gpsimd_rows(r0)
            store(stored[0], stored[1])
